import numpy as np
import ml_dtypes


def mxq(x, axis, fmt="e4m3"):
    dtype, down = {"e4m3": (ml_dtypes.float8_e4m3fn, 7), "e5m2": (ml_dtypes.float8_e5m2, 14)}[fmt]
    v = np.moveaxis(np.asarray(x, np.float32).astype(ml_dtypes.bfloat16).astype(np.float64), axis, -1)
    blocks = v.reshape(v.shape[:-1] + (-1, 32))
    amax = np.abs(blocks).max(-1, keepdims=True)
    byte = np.maximum(np.where(amax > 0, np.frexp(amax)[1] - 1 + 127, 0) - down, 1)
    scale = np.exp2(byte - 127.0)
    codes = (blocks / scale).astype(np.float32).astype(dtype).astype(np.float64)
    return np.moveaxis((codes * scale).reshape(v.shape), -1, axis)


WIDE = False


def mx_kscale(k):
    if not WIDE:
        return np.ones(k)
    levels = np.array([10, -10, 5, -5, 0])
    a = np.random.permutation(np.resize(levels, k // 512 * 4)).reshape(k // 512, 4)
    idx = np.arange(k)
    return np.exp2(a[idx // 512, idx % 128 // 32])


BF16 = ml_dtypes.bfloat16


def bf(x):
    return np.asarray(x, np.float32).astype(BF16)


def f64(x):
    return np.asarray(x).astype(np.float64)


E2M1 = np.array([0.0, 0.5, 1.0, 1.5, 2.0, 3.0, 4.0, 6.0, -0.0, -0.5, -1.0, -1.5, -2.0, -3.0, -4.0, -6.0])


def pack_weight(w, fmt):
    k, n = w.shape
    w = f64(bf(w)).reshape(k // 32, 32, n)
    amax = np.abs(w).max(1)
    if fmt == "e4m3":
        byte = np.frexp(amax)[1] - 1 + 127 - 7
    else:
        mant, ex = np.frexp(amax / 6.0)
        byte = np.where(mant > 0.5, ex, ex - 1) + 127
    byte = np.clip(np.where(amax > 0, byte, 1), 1, 254)
    scaled = (w * np.exp2(127.0 - byte)[:, None, :]).reshape(k, n).astype(np.float32)
    by_word = np.ascontiguousarray(scaled.reshape(k // 512, 128, 4, n).transpose(0, 1, 3, 2))
    if fmt == "e4m3":
        words = by_word.astype(ml_dtypes.float8_e4m3fn).view(np.uint8)
    else:
        c = by_word.astype(ml_dtypes.float4_e2m1fn).view(np.uint8) & 0xF
        words = c[..., 0::2] | (c[..., 1::2] << 4)
    return np.ascontiguousarray(words), np.ascontiguousarray(byte.astype(np.uint8).reshape(k // 512, 16, n))


def unpack_weight(words, scales, fmt):
    g, p, n, _ = words.shape
    if fmt == "e4m3":
        vals = np.ascontiguousarray(words).view(ml_dtypes.float8_e4m3fn).astype(np.float64)
    else:
        nib = np.empty((g, p, n, 4), np.uint8)
        nib[..., 0::2] = words & 0xF
        nib[..., 1::2] = words >> 4
        vals = E2M1[nib]
    vals = vals * np.repeat(np.exp2(scales.astype(np.float64) - 127.0), 8, axis=1)[..., None]
    return vals.transpose(0, 1, 3, 2).reshape(g * 512, n)


B, C, S, OUT = 128, 4, 32, 4096
IN = C * S * S
HS = S // 2
SUB, BLK = 4, 32


def haar_dwt2_features(x):
    x4 = x.reshape(x.shape[0], C, S, S)
    a = x4[:, :, 0::2, 0::2]
    bq = x4[:, :, 0::2, 1::2]
    c = x4[:, :, 1::2, 0::2]
    d = x4[:, :, 1::2, 1::2]
    LL = (a + bq + c + d) * 0.5
    LH = (a + bq - c - d) * 0.5
    HL = (a - bq + c - d) * 0.5
    HH = (a - bq - c + d) * 0.5
    t = np.stack([LL, LH, HL, HH], axis=2)
    return t.reshape(x.shape[0], -1)


def setup_inputs():
    g = mx_kscale(IN).reshape(-1, SUB, BLK)[:, 0, :].reshape(C, HS, HS)
    gx = np.repeat(np.repeat(g, 2, axis=1), 2, axis=2).reshape(IN)
    gt = np.repeat(g[:, None], SUB, axis=1).reshape(IN)
    x = bf(np.random.standard_normal((B, IN)) * gx)
    w = np.random.standard_normal((OUT, IN)) * (1.0 / np.sqrt(IN)) / gt
    words, scales = pack_weight(np.ascontiguousarray(w.T), "e4m3")
    b = bf(np.random.standard_normal(OUT) * 0.5)
    return {"x": x, "W_words": words, "W_scales": scales, "b": b}


def reference(x, W_words, W_scales, b):
    t = haar_dwt2_features(f64(x))
    return (mxq(t, 1, "e4m3") @ unpack_weight(W_words, W_scales, "e4m3")) + f64(b)

@@ -1,0 +1,119 @@
+from contextlib import ExitStack
+
+import concourse.mybir as mybir
+from concourse.masks import make_identity
+
+BF16 = mybir.dt.bfloat16
+F32 = mybir.dt.float32
+I32 = mybir.dt.int32
+U32 = mybir.dt.uint32
+U8 = mybir.dt.uint8
+FP8X4 = mybir.dt.float8_e4m3fn_x4
+ALU = mybir.AluOpType
+ACT = mybir.ActivationFunctionType
+
+P = 128
+CH = 4
+PIX = 1024
+G = 8
+NT = 8
+N_TILE = 512
+OUT = 4096
+
+FLOPS = 2 * 128 * 4096 * 4096
+
+
+def tile_waveletlinearlayer_w_kernel(tc, x, W_words, W_scales, b, out):
+    nc = tc.nc
+    with ExitStack() as ctx:
+        keep = ctx.enter_context(tc.tile_pool(name="keep", bufs=1))
+        psum = ctx.enter_context(tc.psum_pool(name="psum", bufs=1))
+
+        b8 = keep.tile([P, N_TILE], BF16, name="b8")
+        planes = [keep.tile([P, OUT], U8, name="planes%d" % a, align_bytes=64) for a in range(2)]
+        nc.vector.memset(b8[:].bitcast(I32), 0)
+        for a in range(2):
+            nc.vector.memset(planes[a][:].bitcast(I32), 0)
+
+        x_ch = []
+        for ch in range(CH):
+            xt = keep.tile([P, PIX], BF16, name="x%d" % ch)
+            nc.sync.dma_start(out=xt[:], in_=x[:, ch * PIX : (ch + 1) * PIX])
+            x_ch.append(xt)
+        nc.scalar.dma_start(out=b8[0:NT, :], in_=b.rearrange("(j n) -> j n", j=NT))
+        for a in range(2):
+            for q in range(4):
+                nc.sync.dma_start(
+                    out=planes[a][32 * q : 32 * q + 16, :].bitcast(I32),
+                    in_=W_scales[4 * a : 4 * a + 4, 4 * q : 4 * q + 4, :].bitcast(I32),
+                )
+        w_sb = []
+        for g in range(G - 1):
+            wt = keep.tile([P, OUT], I32, name="w%d" % g, align_bytes=64)
+            nc.sync.dma_start(out=wt[:], in_=W_words[g].rearrange("p n t -> p (n t)").bitcast(I32))
+            w_sb.append(wt)
+        w_last = []
+        for j in range(NT):
+            wt = keep.tile([P, N_TILE], I32, name="wl%d" % j, align_bytes=64)
+            nc.sync.dma_start(
+                out=wt[:],
+                in_=W_words[G - 1, :, j * N_TILE : (j + 1) * N_TILE, :].rearrange("p n t -> p (n t)").bitcast(I32),
+            )
+            w_last.append(wt)
+
+        ident = keep.tile([P, P], BF16, name="ident")
+        make_identity(nc, ident[:])
+        bias_sb = keep.tile([P, NT, N_TILE], F32, name="bias_sb")
+        for j in range(NT):
+            pb = psum.tile([P, N_TILE], F32, name="pb%d" % j, tag="bank%d" % j)
+            nc.tensor.matmul(
+                out=pb[:], lhsT=ident[:, j : j + 1].to_broadcast([P, P]), rhs=b8[:], start=True, stop=True
+            )
+            nc.scalar.copy(out=bias_sb[:, j, :], in_=pb[:])
+
+        grouped = keep.tile([P, G, P, 4], BF16, name="grouped", align_bytes=64)
+        t_codes = keep.tile([P, G, P], U32, name="t_codes", align_bytes=64)
+        t_scales = keep.tile([P, G, P], U8, name="t_scales", align_bytes=64)
+        for ch in range(CH):
+            xv = x_ch[ch][:].rearrange("p (w e) -> p e w", e=2)
+            sd = keep.tile([P, 2, PIX // 2], F32, name="sd%d" % ch)
+            nc.vector.tensor_tensor(out=sd[:, 0, :], in0=xv[:, 0, :], in1=xv[:, 1, :], op=ALU.add)
+            nc.vector.tensor_tensor(out=sd[:, 1, :], in0=xv[:, 0, :], in1=xv[:, 1, :], op=ALU.subtract)
+            sv = sd[:].rearrange("p h (i r j) -> p r h i j", r=2, j=16)
+            t2 = keep.tile([P, PIX], BF16, name="t2_%d" % ch)
+            tv = t2[:].rearrange("p (h v i j) -> p v h i j", h=2, v=2, j=16)
+            nc.vector.tensor_tensor(out=tv[:, 0], in0=sv[:, 0], in1=sv[:, 1], op=ALU.add)
+            nc.vector.tensor_tensor(out=tv[:, 1], in0=sv[:, 0], in1=sv[:, 1], op=ALU.subtract)
+            for h in range(2):
+                g = 2 * ch + h
+                pt = psum.tile([P, 4, P], BF16, name="pt%d" % g, tag="bank%d" % g)
+                for t in range(4):
+                    nc.tensor.transpose(pt[:, t, :], t2[:, 512 * h + t : 512 * (h + 1) : 4], ident[:])
+                nc.scalar.activation(
+                    out=grouped[:, g], in_=pt[:].rearrange("p t r -> p r t"), func=ACT.Copy, scale=0.5
+                )
+            nc.vector.quantize_mx(
+                out=t_codes[:, 2 * ch : 2 * ch + 2, :].rearrange("p g r -> p (g r)").bitcast(FP8X4),
+                scales=t_scales[:, 2 * ch : 2 * ch + 2, :].rearrange("p g r -> p (g r)"),
+                in_=grouped[:, 2 * ch : 2 * ch + 2].rearrange("p g r t -> p (g r t)"),
+            )
+
+        acc = [psum.tile([P, N_TILE], F32, name="acc%d" % j, tag="bank%d" % j) for j in range(NT)]
+        for g in range(G):
+            k = 4 * (g % 4)
+            for j in range(NT):
+                cols = slice(j * N_TILE, (j + 1) * N_TILE)
+                rhs = w_sb[g][:, cols] if g < G - 1 else w_last[j][:]
+                nc.tensor.matmul_mx(
+                    out=acc[j][:],
+                    lhsT=t_codes[:, g, :].bitcast(FP8X4),
+                    lhsT_scale=t_scales[:, g, :],
+                    rhs=rhs.bitcast(FP8X4),
+                    rhs_scale=planes[g // 4][k:P, cols],
+                    start=(g == 0),
+                    stop=(g == G - 1),
+                )
+        for j in range(NT):
+            res = keep.tile([P, N_TILE], F32, name="res%d" % j)
+            nc.vector.tensor_tensor(out=res[:], in0=acc[j][:], in1=bias_sb[:, j, :], op=ALU.add)
+            nc.sync.dma_start(out=out[:, j * N_TILE : (j + 1) * N_TILE], in_=res[:])

@@ -35,11 +35,8 @@ def tile_waveletlinearlayer_w_kernel(tc, x, W_words, W_scales, b, out):
         for a in range(2):
             nc.vector.memset(planes[a][:].bitcast(I32), 0)
 
-        x_ch = []
-        for ch in range(CH):
-            xt = keep.tile([P, PIX], BF16, name="x%d" % ch)
-            nc.sync.dma_start(out=xt[:], in_=x[:, ch * PIX : (ch + 1) * PIX])
-            x_ch.append(xt)
+        x_sb = keep.tile([P, CH * PIX], BF16, name="x_sb")
+        nc.sync.dma_start(out=x_sb[:], in_=x)
         nc.scalar.dma_start(out=b8[0:NT, :], in_=b.rearrange("(j n) -> j n", j=NT))
         for a in range(2):
             for q in range(4):
@@ -47,19 +44,17 @@ def tile_waveletlinearlayer_w_kernel(tc, x, W_words, W_scales, b, out):
                     out=planes[a][32 * q : 32 * q + 16, :].bitcast(I32),
                     in_=W_scales[4 * a : 4 * a + 4, 4 * q : 4 * q + 4, :].bitcast(I32),
                 )
+        pieces = [(g, 0, NT) for g in range(G - 2)]
+        pieces += [(G - 2, 0, NT // 2), (G - 1, 0, NT // 2), (G - 2, NT // 2, NT // 2)]
+        pieces += [(G - 1, NT // 2, 2), (G - 1, NT // 2 + 2, 1), (G - 1, NT // 2 + 3, 1)]
         w_sb = []
-        for g in range(G - 1):
-            wt = keep.tile([P, OUT], I32, name="w%d" % g, align_bytes=64)
-            nc.sync.dma_start(out=wt[:], in_=W_words[g].rearrange("p n t -> p (n t)").bitcast(I32))
-            w_sb.append(wt)
-        w_last = []
-        for j in range(NT):
-            wt = keep.tile([P, N_TILE], I32, name="wl%d" % j, align_bytes=64)
+        for g, j0, nj in pieces:
+            wt = keep.tile([P, nj * N_TILE], I32, name="w%d_%d" % (g, j0), align_bytes=64)
             nc.sync.dma_start(
                 out=wt[:],
-                in_=W_words[G - 1, :, j * N_TILE : (j + 1) * N_TILE, :].rearrange("p n t -> p (n t)").bitcast(I32),
+                in_=W_words[g, :, j0 * N_TILE : (j0 + nj) * N_TILE, :].rearrange("p n t -> p (n t)").bitcast(I32),
             )
-            w_last.append(wt)
+            w_sb.append(wt)
 
         ident = keep.tile([P, P], BF16, name="ident")
         make_identity(nc, ident[:])
@@ -75,7 +70,7 @@ def tile_waveletlinearlayer_w_kernel(tc, x, W_words, W_scales, b, out):
         t_codes = keep.tile([P, G, P], U32, name="t_codes", align_bytes=64)
         t_scales = keep.tile([P, G, P], U8, name="t_scales", align_bytes=64)
         for ch in range(CH):
-            xv = x_ch[ch][:].rearrange("p (w e) -> p e w", e=2)
+            xv = x_sb[:, ch * PIX : (ch + 1) * PIX].rearrange("p (w e) -> p e w", e=2)
             sd = keep.tile([P, 2, PIX // 2], F32, name="sd%d" % ch)
             nc.vector.tensor_tensor(out=sd[:, 0, :], in0=xv[:, 0, :], in1=xv[:, 1, :], op=ALU.add)
             nc.vector.tensor_tensor(out=sd[:, 1, :], in0=xv[:, 0, :], in1=xv[:, 1, :], op=ALU.subtract)
@@ -99,21 +94,25 @@ def tile_waveletlinearlayer_w_kernel(tc, x, W_words, W_scales, b, out):
             )
 
         acc = [psum.tile([P, N_TILE], F32, name="acc%d" % j, tag="bank%d" % j) for j in range(NT)]
-        for g in range(G):
+        for (g, j0, nj), wt in zip(pieces, w_sb):
             k = 4 * (g % 4)
-            for j in range(NT):
-                cols = slice(j * N_TILE, (j + 1) * N_TILE)
-                rhs = w_sb[g][:, cols] if g < G - 1 else w_last[j][:]
+            for i in range(nj):
+                j = j0 + i
                 nc.tensor.matmul_mx(
                     out=acc[j][:],
                     lhsT=t_codes[:, g, :].bitcast(FP8X4),
                     lhsT_scale=t_scales[:, g, :],
-                    rhs=rhs.bitcast(FP8X4),
-                    rhs_scale=planes[g // 4][k:P, cols],
+                    rhs=wt[:, i * N_TILE : (i + 1) * N_TILE].bitcast(FP8X4),
+                    rhs_scale=planes[g // 4][k:P, j * N_TILE : (j + 1) * N_TILE],
                     start=(g == 0),
                     stop=(g == G - 1),
                 )
-        for j in range(NT):
-            res = keep.tile([P, N_TILE], F32, name="res%d" % j)
-            nc.vector.tensor_tensor(out=res[:], in0=acc[j][:], in1=bias_sb[:, j, :], op=ALU.add)
-            nc.sync.dma_start(out=out[:, j * N_TILE : (j + 1) * N_TILE], in_=res[:])
+            if g == G - 1:
+                res = keep.tile([P, nj, N_TILE], F32, name="res%d" % j0)
+                for i in range(nj):
+                    nc.vector.tensor_tensor(
+                        out=res[:, i, :], in0=acc[j0 + i][:], in1=bias_sb[:, j0 + i, :], op=ALU.add
+                    )
+                nc.sync.dma_start(
+                    out=out[:, j0 * N_TILE : (j0 + nj) * N_TILE], in_=res[:].rearrange("p j n -> p (j n)")
+                )

@@ -38,8 +38,8 @@ def tile_waveletlinearlayer_w_kernel(tc, x, W_words, W_scales, b, out):
         x_sb = keep.tile([P, CH * PIX], BF16, name="x_sb")
         nc.sync.dma_start(out=x_sb[:], in_=x)
         nc.scalar.dma_start(out=b8[0:NT, :], in_=b.rearrange("(j n) -> j n", j=NT))
-        for a in range(2):
-            for q in range(4):
+        for qs in ((2, 3), (0, 1)):
+            for a, q in ((a, q) for a in range(2) for q in qs):
                 nc.sync.dma_start(
                     out=planes[a][32 * q : 32 * q + 16, :].bitcast(I32),
                     in_=W_scales[4 * a : 4 * a + 4, 4 * q : 4 * q + 4, :].bitcast(I32),

@@ -38,21 +38,24 @@ def tile_waveletlinearlayer_w_kernel(tc, x, W_words, W_scales, b, out):
         x_sb = keep.tile([P, CH * PIX], BF16, name="x_sb")
         nc.sync.dma_start(out=x_sb[:], in_=x)
         nc.scalar.dma_start(out=b8[0:NT, :], in_=b.rearrange("(j n) -> j n", j=NT))
-        for qs in ((2, 3), (0, 1)):
-            for a, q in ((a, q) for a in range(2) for q in qs):
-                nc.sync.dma_start(
-                    out=planes[a][32 * q : 32 * q + 16, :].bitcast(I32),
-                    in_=W_scales[4 * a : 4 * a + 4, 4 * q : 4 * q + 4, :].bitcast(I32),
-                )
-        pieces = [(g, 0, NT) for g in range(G - 2)]
-        pieces += [(G - 2, 0, NT // 2), (G - 1, 0, NT // 2), (G - 2, NT // 2, NT // 2)]
-        pieces += [(G - 1, NT // 2, 2), (G - 1, NT // 2 + 2, 1), (G - 1, NT // 2 + 3, 1)]
+        scale_loads = [(a, q, 0, OUT) for qs in ((2, 3), (0, 1)) for a in range(2) for q in qs]
+        scale_loads[7:] = [(1, 1, 0, OUT // 2), (1, 1, OUT // 2, OUT)]
+        for a, q, c0, c1 in scale_loads:
+            nc.sync.dma_start(
+                out=planes[a][32 * q : 32 * q + 16, c0:c1].bitcast(I32),
+                in_=W_scales[4 * a : 4 * a + 4, 4 * q : 4 * q + 4, c0:c1].bitcast(I32),
+            )
+        pieces = [(0, 2, 0, NT), (2, 2, 0, NT), (4, 1, 0, NT), (5, 3, 0, NT // 2)]
+        pieces += [(5, 1, NT // 2, NT // 2), (6, 1, NT // 2, NT // 2)]
+        pieces += [(7, 1, NT // 2, 2), (7, 1, NT // 2 + 2, 1), (7, 1, NT // 2 + 3, 1)]
         w_sb = []
-        for g, j0, nj in pieces:
-            wt = keep.tile([P, nj * N_TILE], I32, name="w%d_%d" % (g, j0), align_bytes=64)
+        for g0, ng, j0, nj in pieces:
+            wt = keep.tile([P, ng, nj * N_TILE], I32, name="w%d_%d" % (g0, j0), align_bytes=64)
             nc.sync.dma_start(
                 out=wt[:],
-                in_=W_words[g, :, j0 * N_TILE : (j0 + nj) * N_TILE, :].rearrange("p n t -> p (n t)").bitcast(I32),
+                in_=W_words[g0 : g0 + ng, :, j0 * N_TILE : (j0 + nj) * N_TILE, :]
+                .rearrange("g p n t -> p g (n t)")
+                .bitcast(I32),
             )
             w_sb.append(wt)
 
@@ -94,20 +97,21 @@ def tile_waveletlinearlayer_w_kernel(tc, x, W_words, W_scales, b, out):
             )
 
         acc = [psum.tile([P, N_TILE], F32, name="acc%d" % j, tag="bank%d" % j) for j in range(NT)]
-        for (g, j0, nj), wt in zip(pieces, w_sb):
-            k = 4 * (g % 4)
-            for i in range(nj):
-                j = j0 + i
-                nc.tensor.matmul_mx(
-                    out=acc[j][:],
-                    lhsT=t_codes[:, g, :].bitcast(FP8X4),
-                    lhsT_scale=t_scales[:, g, :],
-                    rhs=wt[:, i * N_TILE : (i + 1) * N_TILE].bitcast(FP8X4),
-                    rhs_scale=planes[g // 4][k:P, j * N_TILE : (j + 1) * N_TILE],
-                    start=(g == 0),
-                    stop=(g == G - 1),
-                )
-            if g == G - 1:
+        for (g0, ng, j0, nj), wt in zip(pieces, w_sb):
+            for g in range(g0, g0 + ng):
+                k = 4 * (g % 4)
+                for i in range(nj):
+                    j = j0 + i
+                    nc.tensor.matmul_mx(
+                        out=acc[j][:],
+                        lhsT=t_codes[:, g, :].bitcast(FP8X4),
+                        lhsT_scale=t_scales[:, g, :],
+                        rhs=wt[:, g - g0, i * N_TILE : (i + 1) * N_TILE].bitcast(FP8X4),
+                        rhs_scale=planes[g // 4][k:P, j * N_TILE : (j + 1) * N_TILE],
+                        start=(g == 0),
+                        stop=(g == G - 1),
+                    )
+            if g0 + ng == G:
                 res = keep.tile([P, nj, N_TILE], F32, name="res%d" % j0)
                 for i in range(nj):
                     nc.vector.tensor_tensor(

@@ -38,16 +38,16 @@ def tile_waveletlinearlayer_w_kernel(tc, x, W_words, W_scales, b, out):
         x_sb = keep.tile([P, CH * PIX], BF16, name="x_sb")
         nc.sync.dma_start(out=x_sb[:], in_=x)
         nc.scalar.dma_start(out=b8[0:NT, :], in_=b.rearrange("(j n) -> j n", j=NT))
-        scale_loads = [(a, q, 0, OUT) for qs in ((2, 3), (0, 1)) for a in range(2) for q in qs]
-        scale_loads[7:] = [(1, 1, 0, OUT // 2), (1, 1, OUT // 2, OUT)]
-        for a, q, c0, c1 in scale_loads:
+        for a, q in ((a, q) for qs in ((2, 3), (0, 1)) for a in range(2) for q in qs):
             nc.sync.dma_start(
-                out=planes[a][32 * q : 32 * q + 16, c0:c1].bitcast(I32),
-                in_=W_scales[4 * a : 4 * a + 4, 4 * q : 4 * q + 4, c0:c1].bitcast(I32),
+                out=planes[a][32 * q : 32 * q + 16, :].bitcast(I32),
+                in_=W_scales[4 * a : 4 * a + 4, 4 * q : 4 * q + 4, :].bitcast(I32),
             )
-        pieces = [(0, 2, 0, NT), (2, 2, 0, NT), (4, 1, 0, NT), (5, 3, 0, NT // 2)]
-        pieces += [(5, 1, NT // 2, NT // 2), (6, 1, NT // 2, NT // 2)]
-        pieces += [(7, 1, NT // 2, 2), (7, 1, NT // 2 + 2, 1), (7, 1, NT // 2 + 3, 1)]
+        pieces = [(0, 2, 0, NT), (2, 2, 0, NT), (4, 1, 0, NT)]
+        pieces += [(5, 1, 0, NT // 2), (6, 1, 0, NT // 2), (7, 1, 0, NT // 2)]
+        pieces += [(5, 1, NT // 2, NT // 2)]
+        pieces += [(6, 2, j, 1) for j in range(NT // 2, NT - 1)]
+        pieces += [(g, 1, NT - 1, 1) for g in (6, 7)]
         w_sb = []
         for g0, ng, j0, nj in pieces:
             wt = keep.tile([P, ng, nj * N_TILE], I32, name="w%d_%d" % (g0, j0), align_bytes=64)

@@ -38,10 +38,12 @@ def tile_waveletlinearlayer_w_kernel(tc, x, W_words, W_scales, b, out):
         x_sb = keep.tile([P, CH * PIX], BF16, name="x_sb")
         nc.sync.dma_start(out=x_sb[:], in_=x)
         nc.scalar.dma_start(out=b8[0:NT, :], in_=b.rearrange("(j n) -> j n", j=NT))
-        for a, q in ((a, q) for qs in ((2, 3), (0, 1)) for a in range(2) for q in qs):
+        scale_loads = [(a, q, 0, OUT) for qs in ((2, 3), (0, 1)) for a in range(2) for q in qs]
+        scale_loads[7:] = [(1, 1, 0, OUT // 2), (1, 1, OUT // 2, OUT)]
+        for a, q, c0, c1 in scale_loads:
             nc.sync.dma_start(
-                out=planes[a][32 * q : 32 * q + 16, :].bitcast(I32),
-                in_=W_scales[4 * a : 4 * a + 4, 4 * q : 4 * q + 4, :].bitcast(I32),
+                out=planes[a][32 * q : 32 * q + 16, c0:c1].bitcast(I32),
+                in_=W_scales[4 * a : 4 * a + 4, 4 * q : 4 * q + 4, c0:c1].bitcast(I32),
             )
         pieces = [(0, 2, 0, NT), (2, 2, 0, NT), (4, 1, 0, NT)]
         pieces += [(5, 1, 0, NT // 2), (6, 1, 0, NT // 2), (7, 1, 0, NT // 2)]

from contextlib import ExitStack

import concourse.mybir as mybir
from concourse.masks import make_identity

BF16 = mybir.dt.bfloat16
F32 = mybir.dt.float32
I32 = mybir.dt.int32
U32 = mybir.dt.uint32
U8 = mybir.dt.uint8
FP8X4 = mybir.dt.float8_e4m3fn_x4
ALU = mybir.AluOpType
ACT = mybir.ActivationFunctionType

P = 128
CH = 4
PIX = 1024
G = 8
NT = 8
N_TILE = 512
OUT = 4096

FLOPS = 2 * 128 * 4096 * 4096


def tile_waveletlinearlayer_w_kernel(tc, x, W_words, W_scales, b, out):
    nc = tc.nc
    with ExitStack() as ctx:
        keep = ctx.enter_context(tc.tile_pool(name="keep", bufs=1))
        psum = ctx.enter_context(tc.psum_pool(name="psum", bufs=1))

        b8 = keep.tile([P, N_TILE], BF16, name="b8")
        planes = [keep.tile([P, OUT], U8, name="planes%d" % a, align_bytes=64) for a in range(2)]
        nc.vector.memset(b8[:].bitcast(I32), 0)
        for a in range(2):
            nc.vector.memset(planes[a][:].bitcast(I32), 0)

        x_sb = keep.tile([P, CH * PIX], BF16, name="x_sb")
        nc.sync.dma_start(out=x_sb[:], in_=x)
        nc.scalar.dma_start(out=b8[0:NT, :], in_=b.rearrange("(j n) -> j n", j=NT))
        scale_loads = [(a, q, 0, OUT) for qs in ((2, 3), (0, 1)) for a in range(2) for q in qs]
        scale_loads[7:] = [(1, 1, 0, OUT // 2), (1, 1, OUT // 2, OUT)]
        for a, q, c0, c1 in scale_loads:
            nc.sync.dma_start(
                out=planes[a][32 * q : 32 * q + 16, c0:c1].bitcast(I32),
                in_=W_scales[4 * a : 4 * a + 4, 4 * q : 4 * q + 4, c0:c1].bitcast(I32),
            )
        pieces = [(0, 2, 0, NT), (2, 2, 0, NT), (4, 1, 0, NT)]
        pieces += [(5, 1, 0, NT // 2), (6, 1, 0, NT // 2), (7, 1, 0, NT // 2)]
        pieces += [(5, 1, NT // 2, NT // 2)]
        pieces += [(6, 2, j, 1) for j in range(NT // 2, NT - 1)]
        pieces += [(g, 1, NT - 1, 1) for g in (6, 7)]
        w_sb = []
        for g0, ng, j0, nj in pieces:
            wt = keep.tile([P, ng, nj * N_TILE], I32, name="w%d_%d" % (g0, j0), align_bytes=64)
            nc.sync.dma_start(
                out=wt[:],
                in_=W_words[g0 : g0 + ng, :, j0 * N_TILE : (j0 + nj) * N_TILE, :]
                .rearrange("g p n t -> p g (n t)")
                .bitcast(I32),
            )
            w_sb.append(wt)

        ident = keep.tile([P, P], BF16, name="ident")
        make_identity(nc, ident[:])
        bias_sb = keep.tile([P, NT, N_TILE], F32, name="bias_sb")
        for j in range(NT):
            pb = psum.tile([P, N_TILE], F32, name="pb%d" % j, tag="bank%d" % j)
            nc.tensor.matmul(
                out=pb[:], lhsT=ident[:, j : j + 1].to_broadcast([P, P]), rhs=b8[:], start=True, stop=True
            )
            nc.scalar.copy(out=bias_sb[:, j, :], in_=pb[:])

        grouped = keep.tile([P, G, P, 4], BF16, name="grouped", align_bytes=64)
        t_codes = keep.tile([P, G, P], U32, name="t_codes", align_bytes=64)
        t_scales = keep.tile([P, G, P], U8, name="t_scales", align_bytes=64)
        for ch in range(CH):
            xv = x_sb[:, ch * PIX : (ch + 1) * PIX].rearrange("p (w e) -> p e w", e=2)
            sd = keep.tile([P, 2, PIX // 2], F32, name="sd%d" % ch)
            nc.vector.tensor_tensor(out=sd[:, 0, :], in0=xv[:, 0, :], in1=xv[:, 1, :], op=ALU.add)
            nc.vector.tensor_tensor(out=sd[:, 1, :], in0=xv[:, 0, :], in1=xv[:, 1, :], op=ALU.subtract)
            sv = sd[:].rearrange("p h (i r j) -> p r h i j", r=2, j=16)
            t2 = keep.tile([P, PIX], BF16, name="t2_%d" % ch)
            tv = t2[:].rearrange("p (h v i j) -> p v h i j", h=2, v=2, j=16)
            nc.vector.tensor_tensor(out=tv[:, 0], in0=sv[:, 0], in1=sv[:, 1], op=ALU.add)
            nc.vector.tensor_tensor(out=tv[:, 1], in0=sv[:, 0], in1=sv[:, 1], op=ALU.subtract)
            for h in range(2):
                g = 2 * ch + h
                pt = psum.tile([P, 4, P], BF16, name="pt%d" % g, tag="bank%d" % g)
                for t in range(4):
                    nc.tensor.transpose(pt[:, t, :], t2[:, 512 * h + t : 512 * (h + 1) : 4], ident[:])
                nc.scalar.activation(
                    out=grouped[:, g], in_=pt[:].rearrange("p t r -> p r t"), func=ACT.Copy, scale=0.5
                )
            nc.vector.quantize_mx(
                out=t_codes[:, 2 * ch : 2 * ch + 2, :].rearrange("p g r -> p (g r)").bitcast(FP8X4),
                scales=t_scales[:, 2 * ch : 2 * ch + 2, :].rearrange("p g r -> p (g r)"),
                in_=grouped[:, 2 * ch : 2 * ch + 2].rearrange("p g r t -> p (g r t)"),
            )

        acc = [psum.tile([P, N_TILE], F32, name="acc%d" % j, tag="bank%d" % j) for j in range(NT)]
        for (g0, ng, j0, nj), wt in zip(pieces, w_sb):
            for g in range(g0, g0 + ng):
                k = 4 * (g % 4)
                for i in range(nj):
                    j = j0 + i
                    nc.tensor.matmul_mx(
                        out=acc[j][:],
                        lhsT=t_codes[:, g, :].bitcast(FP8X4),
                        lhsT_scale=t_scales[:, g, :],
                        rhs=wt[:, g - g0, i * N_TILE : (i + 1) * N_TILE].bitcast(FP8X4),
                        rhs_scale=planes[g // 4][k:P, j * N_TILE : (j + 1) * N_TILE],
                        start=(g == 0),
                        stop=(g == G - 1),
                    )
            if g0 + ng == G:
                res = keep.tile([P, nj, N_TILE], F32, name="res%d" % j0)
                for i in range(nj):
                    nc.vector.tensor_tensor(
                        out=res[:, i, :], in0=acc[j0 + i][:], in1=bias_sb[:, j0 + i, :], op=ALU.add
                    )
                nc.sync.dma_start(
                    out=out[:, j0 * N_TILE : (j0 + nj) * N_TILE], in_=res[:].rearrange("p j n -> p (j n)")
                )
